import numpy as np
import ml_dtypes


def mxq(x, axis, fmt="e4m3"):
    dtype, down = {"e4m3": (ml_dtypes.float8_e4m3fn, 7), "e5m2": (ml_dtypes.float8_e5m2, 14)}[fmt]
    v = np.moveaxis(np.asarray(x, np.float32).astype(ml_dtypes.bfloat16).astype(np.float64), axis, -1)
    blocks = v.reshape(v.shape[:-1] + (-1, 32))
    amax = np.abs(blocks).max(-1, keepdims=True)
    byte = np.maximum(np.where(amax > 0, np.frexp(amax)[1] - 1 + 127, 0) - down, 1)
    scale = np.exp2(byte - 127.0)
    codes = (blocks / scale).astype(np.float32).astype(dtype).astype(np.float64)
    return np.moveaxis((codes * scale).reshape(v.shape), -1, axis)


WIDE = False


def mx_kscale(k):
    if not WIDE:
        return np.ones(k)
    levels = np.array([10, -10, 5, -5, 0])
    a = np.random.permutation(np.resize(levels, k // 512 * 4)).reshape(k // 512, 4)
    idx = np.arange(k)
    return np.exp2(a[idx // 512, idx % 128 // 32])


BF16 = ml_dtypes.bfloat16


def bf(x):
    return np.asarray(x, np.float32).astype(BF16)


def f64(x):
    return np.asarray(x).astype(np.float64)


B, T, C, HS, DW, DA, DV, DG = 4, 1024, 1024, 64, 512, 128, 128, 224
H = C // HS


def setup_inputs():
    s = mx_kscale(C)
    return {
        "x": bf(np.random.standard_normal((B, T, C)) * s),
        "x_k": bf(np.random.uniform(0.0, 1.0, C)),
        "Wk": bf(np.random.standard_normal((C, C)) / np.sqrt(C) / s[None, :]),
        "k_k": bf(0.71 + 0.1 * np.random.standard_normal(C)),
    }


def reference(x, x_k, Wk, k_k):
    x = f64(x)
    xprev = np.concatenate([np.zeros_like(x[:, :1]), x[:, :-1]], axis=1)
    xx = xprev - x
    xk = x + xx * f64(x_k)
    k = mxq(xk, 2, "e4m3") @ mxq(f64(Wk), 1, "e4m3").T
    kk4 = (k * f64(k_k)).reshape(B, T, H, HS)
    nrm = np.sqrt((kk4 ** 2).sum(-1, keepdims=True))
    kk = (kk4 / np.maximum(nrm, 1e-12)).reshape(B, T, C)
    return kk

@@ -1,0 +1,223 @@
+from contextlib import ExitStack
+
+import concourse.mybir as mybir
+from concourse.masks import make_identity
+
+FP8X4 = mybir.dt.float8_e4m3fn_x4
+BF16 = mybir.dt.bfloat16
+F32 = mybir.dt.float32
+U32 = mybir.dt.uint32
+U8 = mybir.dt.uint8
+ALU = mybir.AluOpType
+ACT = mybir.ActivationFunctionType
+
+P = 128
+B, T, C = 4, 1024, 1024
+HEAD = 64
+HEADS = C // HEAD
+PACK = 4
+K_PASS = P * PACK
+PASSES = C // K_PASS
+BLOCKS = C // P
+TOKEN_TILES = T // P
+N_TILE = 512
+N_TILES = C // N_TILE
+PAIR = 2
+PAIRS = TOKEN_TILES // PAIR
+RUN = 4
+NORM_FLOOR = 1e-12
+
+FLOPS = 2 * B * T * C * C
+
+
+def tile_full_tmix_params_pa_t_kernel(tc, x, x_k, Wk, k_k, out):
+    nc = tc.nc
+    x_view = x.rearrange("b (i p) c -> p b i c", p=P)
+    w_view = Wk.rearrange("(r p) c -> p r c", p=P)
+    out_view = out.rearrange("b (i p) c -> p b i c", p=P)
+
+    with ExitStack() as ctx:
+        keep = ctx.enter_context(tc.tile_pool(name="keep", bufs=1))
+        w_stage = ctx.enter_context(tc.tile_pool(name="w_stage", bufs=2))
+        mix_stage = ctx.enter_context(tc.tile_pool(name="mix_stage", bufs=2))
+        quantised = ctx.enter_context(tc.tile_pool(name="quantised", bufs=2 * PASSES))
+        results = ctx.enter_context(tc.tile_pool(name="results", bufs=4))
+        norms = ctx.enter_context(tc.tile_pool(name="norms", bufs=4))
+        scratch = ctx.enter_context(tc.tile_pool(name="scratch", bufs=2))
+        flipped = ctx.enter_context(tc.psum_pool(name="flipped", bufs=4))
+        products = ctx.enter_context(tc.psum_pool(name="products", bufs=4))
+
+        x_k_rows = keep.tile([P, P], BF16)
+        nc.vector.memset(x_k_rows[:], 0.0)
+        nc.sync.dma_start(out=x_k_rows[0:BLOCKS, :], in_=x_k.rearrange("(b p) -> b p", p=P))
+
+        x_sb = keep.tile([P, B, TOKEN_TILES, C], BF16)
+        w_sb = keep.tile([P, BLOCKS, C], BF16)
+        k_k_bf = keep.tile([P, C], BF16)
+
+        def load_x(s):
+            for g in range(PASSES):
+                cols = slice(g * K_PASS, (g + 1) * K_PASS)
+                nc.sync.dma_start(out=x_sb[:, s, :, cols], in_=x_view[:, s, :, cols])
+
+        load_x(0)
+        for g in range(PASSES):
+            cols = slice(g * K_PASS, (g + 1) * K_PASS)
+            nc.sync.dma_start(out=w_sb[:, :, cols], in_=w_view[:, :, cols])
+        nc.sync.dma_start(out=k_k_bf[:], in_=k_k.partition_broadcast(P))
+        for s in range(1, B):
+            load_x(s)
+
+        ident = keep.tile([P, P], BF16)
+        make_identity(nc, ident[:])
+
+        one = keep.tile([P, 1], F32)
+        nc.vector.memset(one[:], 1.0)
+        nc.scalar.sqrt(out=one[:], in_=one[:])
+
+        x_k_flipped = flipped.tile([P, T], BF16, tag="bank")
+        nc.tensor.transpose(x_k_flipped[:, 0:P], x_k_rows[:], ident[:])
+        mix_prev = keep.tile([P, BLOCKS], F32)
+        mix_here = keep.tile([P, BLOCKS], F32)
+        nc.vector.tensor_copy(out=mix_prev[:], in_=x_k_flipped[:, 0:BLOCKS])
+        nc.vector.tensor_scalar(
+            out=mix_here[:], in0=mix_prev[:], scalar1=-1.0, scalar2=1.0, op0=ALU.mult, op1=ALU.add
+        )
+
+        k_k_f32 = keep.tile([P, C], F32)
+        nc.vector.tensor_copy(out=k_k_f32[:], in_=k_k_bf[:])
+
+        prev_tiles = [keep.tile([P, T], F32, name="prev_%d" % n) for n in range(3)]
+        for prev in prev_tiles:
+            nc.vector.memset(prev[:, 0:8], 0.0)
+
+        w_codes = keep.tile([P, PASSES, C], U32, align_bytes=64)
+        w_scales = keep.tile([P, PASSES, C], U8, align_bytes=64)
+
+        def quantise_weights(g):
+            w_grouped = w_stage.tile([P, C, PACK], BF16, align_bytes=64)
+            for half_bank in range(BLOCKS // 2):
+                w_flipped = flipped.tile([P, T], BF16, tag="bank")
+                for r in range(2):
+                    for j in range(PACK):
+                        slot = r * PACK + j
+                        block = g * PACK + j
+                        nc.tensor.transpose(
+                            w_flipped[:, slot * P : (slot + 1) * P],
+                            w_sb[:, half_bank * 2 + r, block * P : (block + 1) * P],
+                            ident[:],
+                        )
+                nc.scalar.copy(
+                    out=w_grouped[:, half_bank * 2 * P : (half_bank + 1) * 2 * P, :].rearrange(
+                        "p (r o) j -> p r o j", r=2
+                    ),
+                    in_=w_flipped[:].rearrange("p (r j o) -> p r o j", r=2, j=PACK),
+                )
+            nc.vector.quantize_mx(
+                out=w_codes[:, g, :].bitcast(FP8X4),
+                scales=w_scales[:, g, :],
+                in_=w_grouped[:].rearrange("p o j -> p (o j)"),
+            )
+
+        def mix_and_quantise(s, g):
+            planes = mix_stage.tile([P, PACK, T], BF16)
+            for j in range(PACK):
+                block = g * PACK + j
+                x_flipped = flipped.tile([P, T], BF16, tag="bank")
+                for i in range(TOKEN_TILES):
+                    nc.tensor.transpose(
+                        x_flipped[:, i * P : (i + 1) * P],
+                        x_sb[:, s, i, block * P : (block + 1) * P],
+                        ident[:],
+                    )
+                prev = prev_tiles[block % len(prev_tiles)]
+                nc.scalar.activation(
+                    out=prev[:, 1:T],
+                    in_=x_flipped[:, 0 : T - 1],
+                    func=ACT.Copy,
+                    scale=mix_prev[:, block : block + 1],
+                )
+                nc.vector.scalar_tensor_tensor(
+                    out=planes[:, j, :],
+                    in0=x_flipped[:],
+                    scalar=mix_here[:, block : block + 1],
+                    in1=prev[:],
+                    op0=ALU.mult,
+                    op1=ALU.add,
+                )
+            grouped = mix_stage.tile([P, T, PACK], BF16, align_bytes=64)
+            nc.vector.tensor_copy(
+                out=grouped[:].rearrange("p (c i) j -> p c j i", i=RUN),
+                in_=planes[:].rearrange("p j (c i) -> p c j i", i=RUN),
+            )
+            codes = quantised.tile([P, T], U32, align_bytes=64)
+            scales = quantised.tile([P, T], U8, align_bytes=64)
+            nc.vector.quantize_mx(
+                out=codes[:].bitcast(FP8X4),
+                scales=scales[:],
+                in_=grouped[:].rearrange("p t j -> p (t j)"),
+            )
+            return codes, scales
+
+        def project_and_normalise(s, pair, xk_mx):
+            scaled = results.tile([P, PAIR, C], F32)
+            square_sums = norms.tile([P, PAIR, HEADS], F32)
+            for t in range(PAIR):
+                tokens = slice((pair * PAIR + t) * P, (pair * PAIR + t + 1) * P)
+                for n in range(N_TILES):
+                    cols = slice(n * N_TILE, (n + 1) * N_TILE)
+                    acc = products.tile([P, N_TILE], F32)
+                    for g in range(PASSES):
+                        codes, scales = xk_mx[g]
+                        nc.tensor.matmul_mx(
+                            out=acc[:],
+                            lhsT=codes[:, tokens].bitcast(FP8X4),
+                            lhsT_scale=scales[:, tokens],
+                            rhs=w_codes[:, g, cols].bitcast(FP8X4),
+                            rhs_scale=w_scales[:, g, cols],
+                            start=(g == 0),
+                            stop=(g == PASSES - 1),
+                        )
+                    nc.vector.tensor_tensor(
+                        out=scaled[:, t, cols], in0=acc[:], in1=k_k_f32[:, cols], op=ALU.mult
+                    )
+                squares = scratch.tile([P, C], BF16)
+                for h in range(HEADS):
+                    head = slice(h * HEAD, (h + 1) * HEAD)
+                    nc.scalar.activation(
+                        out=squares[:, head],
+                        in_=scaled[:, t, head],
+                        func=ACT.Square,
+                        accum_out=square_sums[:, t, h : h + 1],
+                    )
+            clamped = norms.tile([P, PAIR * HEADS], F32)
+            norm = norms.tile([P, PAIR * HEADS], F32)
+            inverse = norms.tile([P, PAIR * HEADS], F32)
+            nc.vector.tensor_scalar_max(
+                out=clamped[:],
+                in0=square_sums[:].rearrange("p t h -> p (t h)"),
+                scalar1=NORM_FLOOR * NORM_FLOOR,
+            )
+            nc.scalar.sqrt(out=norm[:], in_=clamped[:])
+            nc.vector.reciprocal(out=inverse[:], in_=norm[:])
+            by_head = scaled[:].rearrange("p t (h d) -> p (t h) d", d=HEAD)
+            nc.gpsimd.tensor_tensor(
+                out=by_head,
+                in0=by_head,
+                in1=inverse[:].unsqueeze(2).to_broadcast([P, PAIR * HEADS, HEAD]),
+                op=ALU.mult,
+            )
+            nc.sync.dma_start(
+                out=out_view[:, s, pair * PAIR : (pair + 1) * PAIR, :], in_=scaled[:]
+            )
+
+        xk_mx = {0: [mix_and_quantise(0, g) for g in range(PASSES)]}
+        for g in range(PASSES):
+            quantise_weights(g)
+        for s in range(B):
+            xk_mx[s + 1] = []
+            for g in range(PASSES):
+                if s + 1 < B:
+                    xk_mx[s + 1].append(mix_and_quantise(s + 1, g))
+                for pair in range(g * PAIRS // PASSES, (g + 1) * PAIRS // PASSES):
+                    project_and_normalise(s, pair, xk_mx[s])

@@ -24,6 +24,7 @@ N_TILE = 512
 N_TILES = C // N_TILE
 PAIR = 2
 PAIRS = TOKEN_TILES // PAIR
+PIECE_HEADS = 8
 RUN = 4
 NORM_FLOOR = 1e-12
 
@@ -201,12 +202,14 @@ def tile_full_tmix_params_pa_t_kernel(tc, x, x_k, Wk, k_k, out):
             nc.scalar.sqrt(out=norm[:], in_=clamped[:])
             nc.vector.reciprocal(out=inverse[:], in_=norm[:])
             by_head = scaled[:].rearrange("p t (h d) -> p (t h) d", d=HEAD)
-            nc.gpsimd.tensor_tensor(
-                out=by_head,
-                in0=by_head,
-                in1=inverse[:].unsqueeze(2).to_broadcast([P, PAIR * HEADS, HEAD]),
-                op=ALU.mult,
-            )
+            for piece in range(PAIR * HEADS // PIECE_HEADS):
+                heads = slice(piece * PIECE_HEADS, (piece + 1) * PIECE_HEADS)
+                nc.gpsimd.tensor_tensor(
+                    out=by_head[:, heads, :],
+                    in0=by_head[:, heads, :],
+                    in1=inverse[:, heads].unsqueeze(2).to_broadcast([P, PIECE_HEADS, HEAD]),
+                    op=ALU.mult,
+                )
             nc.sync.dma_start(
                 out=out_view[:, s, pair * PAIR : (pair + 1) * PAIR, :], in_=scaled[:]
             )

@@ -18,15 +18,26 @@ HEADS = C // HEAD
 PACK = 4
 K_PASS = P * PACK
 PASSES = C // K_PASS
-BLOCKS = C // P
-TOKEN_TILES = T // P
+SLABS = C // P
+TILES = T // P
 N_TILE = 512
 N_TILES = C // N_TILE
 PAIR = 2
-PAIRS = TOKEN_TILES // PAIR
 PIECE_HEADS = 8
 RUN = 4
 NORM_FLOOR = 1e-12
+
+SHIFT_LAG = 1
+BLEND_LAG = 2
+W_LAG = 2
+MULTIPLY_LAG = SLABS + W_LAG + BLEND_LAG
+K_K_LAG = MULTIPLY_LAG + 1
+SUMS_LAG = K_K_LAG + 2
+CLAMP_LAG = SUMS_LAG + 1
+ROOT_LAG = CLAMP_LAG + 2
+INVERT_LAG = ROOT_LAG + 1
+NORMALISE_LAG = INVERT_LAG + 1
+TICKS = B * TILES + NORMALISE_LAG
 
 FLOPS = 2 * B * T * C * C
 
@@ -38,11 +49,12 @@ def tile_full_tmix_params_pa_t_kernel(tc, x, x_k, Wk, k_k, out):
     out_view = out.rearrange("b (i p) c -> p b i c", p=P)
 
     with ExitStack() as ctx:
+        ctx.enter_context(tc.manual_schedule())
         keep = ctx.enter_context(tc.tile_pool(name="keep", bufs=1))
-        w_stage = ctx.enter_context(tc.tile_pool(name="w_stage", bufs=2))
+        w_stage = ctx.enter_context(tc.tile_pool(name="w_stage", bufs=PASSES))
         mix_stage = ctx.enter_context(tc.tile_pool(name="mix_stage", bufs=2))
         quantised = ctx.enter_context(tc.tile_pool(name="quantised", bufs=2 * PASSES))
-        results = ctx.enter_context(tc.tile_pool(name="results", bufs=4))
+        results = ctx.enter_context(tc.tile_pool(name="results", bufs=6))
         norms = ctx.enter_context(tc.tile_pool(name="norms", bufs=4))
         scratch = ctx.enter_context(tc.tile_pool(name="scratch", bufs=2))
         flipped = ctx.enter_context(tc.psum_pool(name="flipped", bufs=4))
@@ -50,24 +62,24 @@ def tile_full_tmix_params_pa_t_kernel(tc, x, x_k, Wk, k_k, out):
 
         x_k_rows = keep.tile([P, P], BF16)
         nc.vector.memset(x_k_rows[:], 0.0)
-        nc.sync.dma_start(out=x_k_rows[0:BLOCKS, :], in_=x_k.rearrange("(b p) -> b p", p=P))
+        nc.sync.dma_start(out=x_k_rows[0:SLABS, :], in_=x_k.rearrange("(b p) -> b p", p=P))
 
-        x_sb = keep.tile([P, B, TOKEN_TILES, C], BF16)
-        w_sb = keep.tile([P, BLOCKS, C], BF16)
+        x_sb = keep.tile([P, B, TILES, C], BF16)
+        w_sb = keep.tile([P, SLABS, C], BF16)
         k_k_bf = keep.tile([P, C], BF16)
 
-        def load_x(s):
+        def load_sequence(s):
             for g in range(PASSES):
                 cols = slice(g * K_PASS, (g + 1) * K_PASS)
                 nc.sync.dma_start(out=x_sb[:, s, :, cols], in_=x_view[:, s, :, cols])
 
-        load_x(0)
+        load_sequence(0)
         for g in range(PASSES):
             cols = slice(g * K_PASS, (g + 1) * K_PASS)
             nc.sync.dma_start(out=w_sb[:, :, cols], in_=w_view[:, :, cols])
         nc.sync.dma_start(out=k_k_bf[:], in_=k_k.partition_broadcast(P))
         for s in range(1, B):
-            load_x(s)
+            load_sequence(s)
 
         ident = keep.tile([P, P], BF16)
         make_identity(nc, ident[:])
@@ -78,149 +90,220 @@ def tile_full_tmix_params_pa_t_kernel(tc, x, x_k, Wk, k_k, out):
 
         x_k_flipped = flipped.tile([P, T], BF16, tag="bank")
         nc.tensor.transpose(x_k_flipped[:, 0:P], x_k_rows[:], ident[:])
-        mix_prev = keep.tile([P, BLOCKS], F32)
-        mix_here = keep.tile([P, BLOCKS], F32)
-        nc.vector.tensor_copy(out=mix_prev[:], in_=x_k_flipped[:, 0:BLOCKS])
+        mix_prev = keep.tile([P, SLABS], F32)
+        mix_here = keep.tile([P, SLABS], F32)
+        nc.vector.tensor_copy(out=mix_prev[:], in_=x_k_flipped[:, 0:SLABS])
         nc.vector.tensor_scalar(
             out=mix_here[:], in0=mix_prev[:], scalar1=-1.0, scalar2=1.0, op0=ALU.mult, op1=ALU.add
         )
-
-        k_k_f32 = keep.tile([P, C], F32)
-        nc.vector.tensor_copy(out=k_k_f32[:], in_=k_k_bf[:])
 
         prev_tiles = [keep.tile([P, T], F32, name="prev_%d" % n) for n in range(3)]
         for prev in prev_tiles:
             nc.vector.memset(prev[:, 0:8], 0.0)
 
+        k_k_f32 = keep.tile([P, C], F32)
         w_codes = keep.tile([P, PASSES, C], U32, align_bytes=64)
         w_scales = keep.tile([P, PASSES, C], U8, align_bytes=64)
 
+        w_banks, w_grouped = {}, {}
+        x_banks, planes, grouped, xk_mx = {}, {}, {}, {}
+        accs, scaled, square_sums, clamped, norm, inverse = {}, {}, {}, {}, {}, {}
+
+        def flip_weights(b):
+            g, quarter = divmod(b, SLABS // PASSES)
+            w_banks[b] = products.tile([P, T], BF16, tag="acc", name="w_bank")
+            for r in range(2):
+                for j in range(PACK):
+                    slot = r * PACK + j
+                    slab = g * PACK + j
+                    nc.tensor.transpose(
+                        w_banks[b][:, slot * P : (slot + 1) * P],
+                        w_sb[:, quarter * 2 + r, slab * P : (slab + 1) * P],
+                        ident[:],
+                    )
+
+        def group_weights(b):
+            g, quarter = divmod(b, SLABS // PASSES)
+            if quarter == 0:
+                w_grouped[g] = w_stage.tile([P, C, PACK], BF16, align_bytes=64, name="w_grouped")
+            nc.scalar.copy(
+                out=w_grouped[g][:, quarter * 2 * P : (quarter + 1) * 2 * P, :].rearrange(
+                    "p (r o) j -> p r o j", r=2
+                ),
+                in_=w_banks[b][:].rearrange("p (r j o) -> p r o j", r=2, j=PACK),
+            )
+
         def quantise_weights(g):
-            w_grouped = w_stage.tile([P, C, PACK], BF16, align_bytes=64)
-            for half_bank in range(BLOCKS // 2):
-                w_flipped = flipped.tile([P, T], BF16, tag="bank")
-                for r in range(2):
-                    for j in range(PACK):
-                        slot = r * PACK + j
-                        block = g * PACK + j
-                        nc.tensor.transpose(
-                            w_flipped[:, slot * P : (slot + 1) * P],
-                            w_sb[:, half_bank * 2 + r, block * P : (block + 1) * P],
-                            ident[:],
-                        )
-                nc.scalar.copy(
-                    out=w_grouped[:, half_bank * 2 * P : (half_bank + 1) * 2 * P, :].rearrange(
-                        "p (r o) j -> p r o j", r=2
-                    ),
-                    in_=w_flipped[:].rearrange("p (r j o) -> p r o j", r=2, j=PACK),
-                )
             nc.vector.quantize_mx(
                 out=w_codes[:, g, :].bitcast(FP8X4),
                 scales=w_scales[:, g, :],
-                in_=w_grouped[:].rearrange("p o j -> p (o j)"),
+                in_=w_grouped[g][:].rearrange("p o j -> p (o j)"),
             )
 
-        def mix_and_quantise(s, g):
-            planes = mix_stage.tile([P, PACK, T], BF16)
-            for j in range(PACK):
-                block = g * PACK + j
-                x_flipped = flipped.tile([P, T], BF16, tag="bank")
-                for i in range(TOKEN_TILES):
-                    nc.tensor.transpose(
-                        x_flipped[:, i * P : (i + 1) * P],
-                        x_sb[:, s, i, block * P : (block + 1) * P],
-                        ident[:],
-                    )
-                prev = prev_tiles[block % len(prev_tiles)]
-                nc.scalar.activation(
-                    out=prev[:, 1:T],
-                    in_=x_flipped[:, 0 : T - 1],
-                    func=ACT.Copy,
-                    scale=mix_prev[:, block : block + 1],
+        def flip(m):
+            s, slab = divmod(m, SLABS)
+            x_banks[m] = flipped.tile([P, T], BF16, tag="bank", name="x_bank")
+            for i in range(TILES):
+                nc.tensor.transpose(
+                    x_banks[m][:, i * P : (i + 1) * P],
+                    x_sb[:, s, i, slab * P : (slab + 1) * P],
+                    ident[:],
                 )
-                nc.vector.scalar_tensor_tensor(
-                    out=planes[:, j, :],
-                    in0=x_flipped[:],
-                    scalar=mix_here[:, block : block + 1],
-                    in1=prev[:],
-                    op0=ALU.mult,
-                    op1=ALU.add,
-                )
-            grouped = mix_stage.tile([P, T, PACK], BF16, align_bytes=64)
-            nc.vector.tensor_copy(
-                out=grouped[:].rearrange("p (c i) j -> p c j i", i=RUN),
-                in_=planes[:].rearrange("p j (c i) -> p c j i", i=RUN),
+
+        def shift(m):
+            slab = m % SLABS
+            nc.scalar.activation(
+                out=prev_tiles[m % len(prev_tiles)][:, 1:T],
+                in_=x_banks[m][:, 0 : T - 1],
+                func=ACT.Copy,
+                scale=mix_prev[:, slab : slab + 1],
             )
+
+        def blend(m):
+            slab = m % SLABS
+            q, j = divmod(m, PACK)
+            if j == 0:
+                planes[q] = mix_stage.tile([P, PACK, T], BF16, name="planes")
+            nc.vector.scalar_tensor_tensor(
+                out=planes[q][:, j, :],
+                in0=x_banks[m][:],
+                scalar=mix_here[:, slab : slab + 1],
+                in1=prev_tiles[m % len(prev_tiles)][:],
+                op0=ALU.mult,
+                op1=ALU.add,
+            )
+
+        def regroup(q):
+            grouped[q] = mix_stage.tile([P, T, PACK], BF16, align_bytes=64, name="grouped")
+            nc.vector.tensor_copy(
+                out=grouped[q][:].rearrange("p (c i) j -> p c j i", i=RUN),
+                in_=planes[q][:].rearrange("p j (c i) -> p c j i", i=RUN),
+            )
+
+        def quantise(q):
             codes = quantised.tile([P, T], U32, align_bytes=64)
             scales = quantised.tile([P, T], U8, align_bytes=64)
             nc.vector.quantize_mx(
                 out=codes[:].bitcast(FP8X4),
                 scales=scales[:],
-                in_=grouped[:].rearrange("p t j -> p (t j)"),
+                in_=grouped[q][:].rearrange("p t j -> p (t j)"),
             )
-            return codes, scales
+            xk_mx[q] = (codes, scales)
 
-        def project_and_normalise(s, pair, xk_mx):
-            scaled = results.tile([P, PAIR, C], F32)
-            square_sums = norms.tile([P, PAIR, HEADS], F32)
-            for t in range(PAIR):
-                tokens = slice((pair * PAIR + t) * P, (pair * PAIR + t + 1) * P)
-                for n in range(N_TILES):
-                    cols = slice(n * N_TILE, (n + 1) * N_TILE)
-                    acc = products.tile([P, N_TILE], F32)
-                    for g in range(PASSES):
-                        codes, scales = xk_mx[g]
-                        nc.tensor.matmul_mx(
-                            out=acc[:],
-                            lhsT=codes[:, tokens].bitcast(FP8X4),
-                            lhsT_scale=scales[:, tokens],
-                            rhs=w_codes[:, g, cols].bitcast(FP8X4),
-                            rhs_scale=w_scales[:, g, cols],
-                            start=(g == 0),
-                            stop=(g == PASSES - 1),
-                        )
-                    nc.vector.tensor_tensor(
-                        out=scaled[:, t, cols], in0=acc[:], in1=k_k_f32[:, cols], op=ALU.mult
+        def multiply(n):
+            s, i = divmod(n, TILES)
+            tokens = slice(i * P, (i + 1) * P)
+            accs[n] = []
+            for half in range(N_TILES):
+                cols = slice(half * N_TILE, (half + 1) * N_TILE)
+                acc = products.tile([P, N_TILE], F32, tag="acc")
+                for g in range(PASSES):
+                    codes, scales = xk_mx[s * PASSES + g]
+                    nc.tensor.matmul_mx(
+                        out=acc[:],
+                        lhsT=codes[:, tokens].bitcast(FP8X4),
+                        lhsT_scale=scales[:, tokens],
+                        rhs=w_codes[:, g, cols].bitcast(FP8X4),
+                        rhs_scale=w_scales[:, g, cols],
+                        start=(g == 0),
+                        stop=(g == PASSES - 1),
                     )
-                squares = scratch.tile([P, C], BF16)
-                for h in range(HEADS):
-                    head = slice(h * HEAD, (h + 1) * HEAD)
-                    nc.scalar.activation(
-                        out=squares[:, head],
-                        in_=scaled[:, t, head],
-                        func=ACT.Square,
-                        accum_out=square_sums[:, t, h : h + 1],
-                    )
-            clamped = norms.tile([P, PAIR * HEADS], F32)
-            norm = norms.tile([P, PAIR * HEADS], F32)
-            inverse = norms.tile([P, PAIR * HEADS], F32)
-            nc.vector.tensor_scalar_max(
-                out=clamped[:],
-                in0=square_sums[:].rearrange("p t h -> p (t h)"),
-                scalar1=NORM_FLOOR * NORM_FLOOR,
-            )
-            nc.scalar.sqrt(out=norm[:], in_=clamped[:])
-            nc.vector.reciprocal(out=inverse[:], in_=norm[:])
-            by_head = scaled[:].rearrange("p t (h d) -> p (t h) d", d=HEAD)
-            for piece in range(PAIR * HEADS // PIECE_HEADS):
-                heads = slice(piece * PIECE_HEADS, (piece + 1) * PIECE_HEADS)
-                nc.gpsimd.tensor_tensor(
-                    out=by_head[:, heads, :],
-                    in0=by_head[:, heads, :],
-                    in1=inverse[:, heads].unsqueeze(2).to_broadcast([P, PIECE_HEADS, HEAD]),
-                    op=ALU.mult,
+                accs[n].append(acc)
+
+        def times_k_k(n):
+            pair, t = divmod(n, PAIR)
+            if t == 0:
+                scaled[pair] = results.tile([P, PAIR, C], F32, name="scaled")
+            for half in range(N_TILES):
+                cols = slice(half * N_TILE, (half + 1) * N_TILE)
+                nc.vector.tensor_tensor(
+                    out=scaled[pair][:, t, cols], in0=accs[n][half][:], in1=k_k_f32[:, cols], op=ALU.mult
                 )
-            nc.sync.dma_start(
-                out=out_view[:, s, pair * PAIR : (pair + 1) * PAIR, :], in_=scaled[:]
+
+        def sum_squares(n):
+            pair, t = divmod(n, PAIR)
+            if t == 0:
+                square_sums[pair] = norms.tile([P, PAIR * HEADS], F32, name="square_sums")
+            squares = scratch.tile([P, C], BF16)
+            for h in range(HEADS):
+                head = slice(h * HEAD, (h + 1) * HEAD)
+                nc.scalar.activation(
+                    out=squares[:, head],
+                    in_=scaled[pair][:, t, head],
+                    func=ACT.Square,
+                    accum_out=square_sums[pair][:, t * HEADS + h : t * HEADS + h + 1],
+                )
+
+        def clamp(pair):
+            clamped[pair] = norms.tile([P, PAIR * HEADS], F32, name="clamped")
+            nc.gpsimd.tensor_scalar_max(
+                out=clamped[pair][:], in0=square_sums[pair][:], scalar1=NORM_FLOOR * NORM_FLOOR
             )
 
-        xk_mx = {0: [mix_and_quantise(0, g) for g in range(PASSES)]}
-        for g in range(PASSES):
-            quantise_weights(g)
-        for s in range(B):
-            xk_mx[s + 1] = []
-            for g in range(PASSES):
-                if s + 1 < B:
-                    xk_mx[s + 1].append(mix_and_quantise(s + 1, g))
-                for pair in range(g * PAIRS // PASSES, (g + 1) * PAIRS // PASSES):
-                    project_and_normalise(s, pair, xk_mx[s])
+        def root(pair):
+            norm[pair] = norms.tile([P, PAIR * HEADS], F32, name="norm")
+            nc.scalar.sqrt(out=norm[pair][:], in_=clamped[pair][:])
+
+        def invert(pair):
+            inverse[pair] = norms.tile([P, PAIR * HEADS], F32, name="inverse")
+            nc.vector.reciprocal(out=inverse[pair][:], in_=norm[pair][:])
+
+        def normalise_and_store(pair, engine):
+            s, first = divmod(pair * PAIR, TILES)
+            by_head = scaled[pair][:].rearrange("p t (h d) -> p (t h) d", d=HEAD)
+            for t in range(PAIR):
+                for piece in range(t * HEADS // PIECE_HEADS, (t + 1) * HEADS // PIECE_HEADS):
+                    heads = slice(piece * PIECE_HEADS, (piece + 1) * PIECE_HEADS)
+                    engine.tensor_tensor(
+                        out=by_head[:, heads, :],
+                        in0=by_head[:, heads, :],
+                        in1=inverse[pair][:, heads].unsqueeze(2).to_broadcast([P, PIECE_HEADS, HEAD]),
+                        op=ALU.mult,
+                    )
+                nc.sync.dma_start(out=out_view[:, s, first + t, :], in_=scaled[pair][:, t, :])
+
+        def due(index, count):
+            return 0 <= index < count
+
+        for tick in range(TICKS):
+            if due(tick, B * SLABS):
+                flip(tick)
+            if due(tick - W_LAG, SLABS):
+                flip_weights(tick - W_LAG)
+            if due(tick - MULTIPLY_LAG, B * TILES):
+                multiply(tick - MULTIPLY_LAG)
+
+            if due(tick - SHIFT_LAG, B * SLABS):
+                shift(tick - SHIFT_LAG)
+            if due(tick - W_LAG - SHIFT_LAG, SLABS):
+                group_weights(tick - W_LAG - SHIFT_LAG)
+
+            m = tick - BLEND_LAG
+            b = tick - W_LAG - BLEND_LAG
+            if due(m, B * SLABS):
+                blend(m)
+                if m % PACK == PACK - 1:
+                    regroup(m // PACK)
+            if tick == MULTIPLY_LAG:
+                nc.vector.tensor_copy(out=k_k_f32[:], in_=k_k_bf[:])
+            if due(tick - K_K_LAG, B * TILES):
+                times_k_k(tick - K_K_LAG)
+            if due(m, B * SLABS) and m % PACK == PACK - 1:
+                quantise(m // PACK)
+            if due(b, SLABS) and b % PACK == PACK - 1:
+                quantise_weights(b // PACK)
+
+            if due(tick - SUMS_LAG, B * TILES):
+                sum_squares(tick - SUMS_LAG)
+
+            if due(tick - CLAMP_LAG, B * TILES) and (tick - CLAMP_LAG) % PAIR == PAIR - 1:
+                clamp((tick - CLAMP_LAG) // PAIR)
+            if due(tick - ROOT_LAG, B * TILES) and (tick - ROOT_LAG) % PAIR == PAIR - 1:
+                root((tick - ROOT_LAG) // PAIR)
+            if due(tick - INVERT_LAG, B * TILES) and (tick - INVERT_LAG) % PAIR == PAIR - 1:
+                invert((tick - INVERT_LAG) // PAIR)
+            if due(tick - NORMALISE_LAG, B * TILES) and (tick - NORMALISE_LAG) % PAIR == PAIR - 1:
+                last_sequence = tick - NORMALISE_LAG >= (B - 1) * TILES
+                normalise_and_store(
+                    (tick - NORMALISE_LAG) // PAIR, nc.vector if last_sequence else nc.gpsimd
+                )

@@ -26,17 +26,15 @@ PAIR = 2
 PIECE_HEADS = 8
 RUN = 4
 NORM_FLOOR = 1e-12
+TINY = 1e-34
 
 SHIFT_LAG = 1
 BLEND_LAG = 2
-W_LAG = 2
+W_LAG = 1
 MULTIPLY_LAG = SLABS + W_LAG + BLEND_LAG
 K_K_LAG = MULTIPLY_LAG + 1
 SUMS_LAG = K_K_LAG + 2
-CLAMP_LAG = SUMS_LAG + 1
-ROOT_LAG = CLAMP_LAG + 2
-INVERT_LAG = ROOT_LAG + 1
-NORMALISE_LAG = INVERT_LAG + 1
+NORMALISE_LAG = SUMS_LAG + 1
 TICKS = B * TILES + NORMALISE_LAG
 
 FLOPS = 2 * B * T * C * C
@@ -67,26 +65,22 @@ def tile_full_tmix_params_pa_t_kernel(tc, x, x_k, Wk, k_k, out):
         x_sb = keep.tile([P, B, TILES, C], BF16)
         w_sb = keep.tile([P, SLABS, C], BF16)
         k_k_bf = keep.tile([P, C], BF16)
-
-        def load_sequence(s):
-            for g in range(PASSES):
-                cols = slice(g * K_PASS, (g + 1) * K_PASS)
-                nc.sync.dma_start(out=x_sb[:, s, :, cols], in_=x_view[:, s, :, cols])
-
-        load_sequence(0)
         for g in range(PASSES):
             cols = slice(g * K_PASS, (g + 1) * K_PASS)
+            nc.sync.dma_start(out=x_sb[:, 0, :, cols], in_=x_view[:, 0, :, cols])
             nc.sync.dma_start(out=w_sb[:, :, cols], in_=w_view[:, :, cols])
         nc.sync.dma_start(out=k_k_bf[:], in_=k_k.partition_broadcast(P))
         for s in range(1, B):
-            load_sequence(s)
+            for g in range(PASSES):
+                cols = slice(g * K_PASS, (g + 1) * K_PASS)
+                nc.sync.dma_start(out=x_sb[:, s, :, cols], in_=x_view[:, s, :, cols])
 
         ident = keep.tile([P, P], BF16)
         make_identity(nc, ident[:])
 
         one = keep.tile([P, 1], F32)
         nc.vector.memset(one[:], 1.0)
-        nc.scalar.sqrt(out=one[:], in_=one[:])
+        nc.scalar.activation(out=one[:], in_=one[:], func=ACT.Abs_reciprocal_sqrt)
 
         x_k_flipped = flipped.tile([P, T], BF16, tag="bank")
         nc.tensor.transpose(x_k_flipped[:, 0:P], x_k_rows[:], ident[:])
@@ -107,7 +101,7 @@ def tile_full_tmix_params_pa_t_kernel(tc, x, x_k, Wk, k_k, out):
 
         w_banks, w_grouped = {}, {}
         x_banks, planes, grouped, xk_mx = {}, {}, {}, {}
-        accs, scaled, square_sums, clamped, norm, inverse = {}, {}, {}, {}, {}, {}
+        accs, scaled, square_sums, inverse = {}, {}, {}, {}
 
         def flip_weights(b):
             g, quarter = divmod(b, SLABS // PASSES)
@@ -234,22 +228,20 @@ def tile_full_tmix_params_pa_t_kernel(tc, x, x_k, Wk, k_k, out):
                     accum_out=square_sums[pair][:, t * HEADS + h : t * HEADS + h + 1],
                 )
 
-        def clamp(pair):
-            clamped[pair] = norms.tile([P, PAIR * HEADS], F32, name="clamped")
-            nc.gpsimd.tensor_scalar_max(
-                out=clamped[pair][:], in0=square_sums[pair][:], scalar1=NORM_FLOOR * NORM_FLOOR
-            )
-
-        def root(pair):
-            norm[pair] = norms.tile([P, PAIR * HEADS], F32, name="norm")
-            nc.scalar.sqrt(out=norm[pair][:], in_=clamped[pair][:])
-
-        def invert(pair):
+        def invert_norms(pair):
             inverse[pair] = norms.tile([P, PAIR * HEADS], F32, name="inverse")
-            nc.vector.reciprocal(out=inverse[pair][:], in_=norm[pair][:])
+            nc.scalar.activation(
+                out=inverse[pair][:],
+                in_=square_sums[pair][:],
+                func=ACT.Abs_reciprocal_sqrt,
+                bias=TINY,
+            )
 
         def normalise_and_store(pair, engine):
             s, first = divmod(pair * PAIR, TILES)
+            engine.tensor_scalar_min(
+                out=inverse[pair][:], in0=inverse[pair][:], scalar1=1.0 / NORM_FLOOR
+            )
             by_head = scaled[pair][:].rearrange("p t (h d) -> p (t h) d", d=HEAD)
             for t in range(PAIR):
                 for piece in range(t * HEADS // PIECE_HEADS, (t + 1) * HEADS // PIECE_HEADS):
@@ -295,13 +287,9 @@ def tile_full_tmix_params_pa_t_kernel(tc, x, x_k, Wk, k_k, out):
 
             if due(tick - SUMS_LAG, B * TILES):
                 sum_squares(tick - SUMS_LAG)
+                if (tick - SUMS_LAG) % PAIR == PAIR - 1:
+                    invert_norms((tick - SUMS_LAG) // PAIR)
 
-            if due(tick - CLAMP_LAG, B * TILES) and (tick - CLAMP_LAG) % PAIR == PAIR - 1:
-                clamp((tick - CLAMP_LAG) // PAIR)
-            if due(tick - ROOT_LAG, B * TILES) and (tick - ROOT_LAG) % PAIR == PAIR - 1:
-                root((tick - ROOT_LAG) // PAIR)
-            if due(tick - INVERT_LAG, B * TILES) and (tick - INVERT_LAG) % PAIR == PAIR - 1:
-                invert((tick - INVERT_LAG) // PAIR)
             if due(tick - NORMALISE_LAG, B * TILES) and (tick - NORMALISE_LAG) % PAIR == PAIR - 1:
                 last_sequence = tick - NORMALISE_LAG >= (B - 1) * TILES
                 normalise_and_store(

@@ -24,6 +24,9 @@ N_TILE = 512
 N_TILES = C // N_TILE
 PAIR = 2
 PIECE_HEADS = 8
+V_HEADS = 4
+S_HEADS = HEADS - V_HEADS
+STATS = 3
 RUN = 4
 NORM_FLOOR = 1e-12
 TINY = 1e-34
@@ -33,6 +36,7 @@ BLEND_LAG = 2
 W_LAG = 1
 MULTIPLY_LAG = SLABS + W_LAG + BLEND_LAG
 K_K_LAG = MULTIPLY_LAG + 1
+V_SUMS_LAG = K_K_LAG + 1
 SUMS_LAG = K_K_LAG + 2
 NORMALISE_LAG = SUMS_LAG + 1
 TICKS = B * TILES + NORMALISE_LAG
@@ -101,7 +105,7 @@ def tile_full_tmix_params_pa_t_kernel(tc, x, x_k, Wk, k_k, out):
 
         w_banks, w_grouped = {}, {}
         x_banks, planes, grouped, xk_mx = {}, {}, {}, {}
-        accs, scaled, square_sums, inverse = {}, {}, {}, {}
+        accs, scaled, stats, v_sums, s_sums, inverse = {}, {}, {}, {}, {}, {}
 
         def flip_weights(b):
             g, quarter = divmod(b, SLABS // PASSES)
@@ -214,34 +218,62 @@ def tile_full_tmix_params_pa_t_kernel(tc, x, x_k, Wk, k_k, out):
                     out=scaled[pair][:, t, cols], in0=accs[n][half][:], in1=k_k_f32[:, cols], op=ALU.mult
                 )
 
-        def sum_squares(n):
+        def sum_squares_on_vector(n):
             pair, t = divmod(n, PAIR)
             if t == 0:
-                square_sums[pair] = norms.tile([P, PAIR * HEADS], F32, name="square_sums")
-            squares = scratch.tile([P, C], BF16)
-            for h in range(HEADS):
-                head = slice(h * HEAD, (h + 1) * HEAD)
-                nc.scalar.activation(
-                    out=squares[:, head],
-                    in_=scaled[pair][:, t, head],
-                    func=ACT.Square,
-                    accum_out=square_sums[pair][:, t * HEADS + h : t * HEADS + h + 1],
+                stats[pair] = norms.tile([P, PAIR, V_HEADS, STATS], F32, name="stats")
+            for h in range(0, V_HEADS, 2):
+                nc.vector.bn_stats(
+                    out=stats[pair][:, t, h : h + 2, :].rearrange("p h k -> p (h k)"),
+                    in_=scaled[pair][:, t, h * HEAD : (h + 2) * HEAD].rearrange(
+                        "p (h d) -> p d h", h=2
+                    ),
                 )
 
-        def invert_norms(pair):
-            inverse[pair] = norms.tile([P, PAIR * HEADS], F32, name="inverse")
-            nc.scalar.activation(
-                out=inverse[pair][:],
-                in_=square_sums[pair][:],
-                func=ACT.Abs_reciprocal_sqrt,
-                bias=TINY,
+        def sum_squares_on_scalar(n):
+            pair, t = divmod(n, PAIR)
+            if t == 0:
+                s_sums[pair] = norms.tile([P, PAIR, S_HEADS], F32, name="s_sums")
+            squares = scratch.tile([P, S_HEADS * HEAD], BF16)
+            for h in range(S_HEADS):
+                nc.scalar.activation(
+                    out=squares[:, h * HEAD : (h + 1) * HEAD],
+                    in_=scaled[pair][:, t, (V_HEADS + h) * HEAD : (V_HEADS + h + 1) * HEAD],
+                    func=ACT.Square,
+                    accum_out=s_sums[pair][:, t, h : h + 1],
+                )
+
+        def finish_vector_sums(pair):
+            mean = stats[pair][:, :, :, 1]
+            mean_squared = norms.tile([P, PAIR, V_HEADS], F32)
+            v_sums[pair] = norms.tile([P, PAIR, V_HEADS], F32, name="v_sums")
+            nc.vector.tensor_tensor(out=mean_squared[:], in0=mean, in1=mean, op=ALU.mult)
+            nc.vector.scalar_tensor_tensor(
+                out=v_sums[pair][:],
+                in0=mean_squared[:],
+                scalar=float(HEAD),
+                in1=stats[pair][:, :, :, 2],
+                op0=ALU.mult,
+                op1=ALU.add,
             )
+
+        def invert_norms(pair):
+            inverse[pair] = norms.tile([P, PAIR, HEADS], F32, name="inverse")
+            for sums, heads in (
+                (v_sums[pair], slice(0, V_HEADS)),
+                (s_sums[pair], slice(V_HEADS, HEADS)),
+            ):
+                nc.scalar.activation(
+                    out=inverse[pair][:, :, heads],
+                    in_=sums[:],
+                    func=ACT.Abs_reciprocal_sqrt,
+                    bias=TINY,
+                )
 
         def normalise_and_store(pair, engine):
             s, first = divmod(pair * PAIR, TILES)
-            engine.tensor_scalar_min(
-                out=inverse[pair][:], in0=inverse[pair][:], scalar1=1.0 / NORM_FLOOR
-            )
+            capped = inverse[pair][:].rearrange("p t h -> p (t h)")
+            engine.tensor_scalar_min(out=capped, in0=capped, scalar1=1.0 / NORM_FLOOR)
             by_head = scaled[pair][:].rearrange("p t (h d) -> p (t h) d", d=HEAD)
             for t in range(PAIR):
                 for piece in range(t * HEADS // PIECE_HEADS, (t + 1) * HEADS // PIECE_HEADS):
@@ -249,7 +281,7 @@ def tile_full_tmix_params_pa_t_kernel(tc, x, x_k, Wk, k_k, out):
                     engine.tensor_tensor(
                         out=by_head[:, heads, :],
                         in0=by_head[:, heads, :],
-                        in1=inverse[pair][:, heads].unsqueeze(2).to_broadcast([P, PIECE_HEADS, HEAD]),
+                        in1=capped[:, heads].unsqueeze(2).to_broadcast([P, PIECE_HEADS, HEAD]),
                         op=ALU.mult,
                     )
                 nc.sync.dma_start(out=out_view[:, s, first + t, :], in_=scaled[pair][:, t, :])
@@ -280,13 +312,17 @@ def tile_full_tmix_params_pa_t_kernel(tc, x, x_k, Wk, k_k, out):
                 nc.vector.tensor_copy(out=k_k_f32[:], in_=k_k_bf[:])
             if due(tick - K_K_LAG, B * TILES):
                 times_k_k(tick - K_K_LAG)
+            if due(tick - V_SUMS_LAG, B * TILES):
+                sum_squares_on_vector(tick - V_SUMS_LAG)
+                if (tick - V_SUMS_LAG) % PAIR == PAIR - 1:
+                    finish_vector_sums((tick - V_SUMS_LAG) // PAIR)
             if due(m, B * SLABS) and m % PACK == PACK - 1:
                 quantise(m // PACK)
             if due(b, SLABS) and b % PACK == PACK - 1:
                 quantise_weights(b // PACK)
 
             if due(tick - SUMS_LAG, B * TILES):
-                sum_squares(tick - SUMS_LAG)
+                sum_squares_on_scalar(tick - SUMS_LAG)
                 if (tick - SUMS_LAG) % PAIR == PAIR - 1:
                     invert_norms((tick - SUMS_LAG) // PAIR)
 

from contextlib import ExitStack

import concourse.mybir as mybir
from concourse.masks import make_identity

FP8X4 = mybir.dt.float8_e4m3fn_x4
BF16 = mybir.dt.bfloat16
F32 = mybir.dt.float32
U32 = mybir.dt.uint32
U8 = mybir.dt.uint8
ALU = mybir.AluOpType
ACT = mybir.ActivationFunctionType

P = 128
B, T, C = 4, 1024, 1024
HEAD = 64
HEADS = C // HEAD
PACK = 4
K_PASS = P * PACK
PASSES = C // K_PASS
SLABS = C // P
TILES = T // P
N_TILE = 512
N_TILES = C // N_TILE
PAIR = 2
PIECE_HEADS = 8
V_HEADS = 4
S_HEADS = HEADS - V_HEADS
STATS = 3
RUN = 4
NORM_FLOOR = 1e-12
TINY = 1e-34

SHIFT_LAG = 1
BLEND_LAG = 2
W_LAG = 1
MULTIPLY_LAG = SLABS + W_LAG + BLEND_LAG
K_K_LAG = MULTIPLY_LAG + 1
V_SUMS_LAG = K_K_LAG + 1
SUMS_LAG = K_K_LAG + 2
NORMALISE_LAG = SUMS_LAG + 1
TICKS = B * TILES + NORMALISE_LAG

FLOPS = 2 * B * T * C * C


def tile_full_tmix_params_pa_t_kernel(tc, x, x_k, Wk, k_k, out):
    nc = tc.nc
    x_view = x.rearrange("b (i p) c -> p b i c", p=P)
    w_view = Wk.rearrange("(r p) c -> p r c", p=P)
    out_view = out.rearrange("b (i p) c -> p b i c", p=P)

    with ExitStack() as ctx:
        ctx.enter_context(tc.manual_schedule())
        keep = ctx.enter_context(tc.tile_pool(name="keep", bufs=1))
        w_stage = ctx.enter_context(tc.tile_pool(name="w_stage", bufs=PASSES))
        mix_stage = ctx.enter_context(tc.tile_pool(name="mix_stage", bufs=2))
        quantised = ctx.enter_context(tc.tile_pool(name="quantised", bufs=2 * PASSES))
        results = ctx.enter_context(tc.tile_pool(name="results", bufs=6))
        norms = ctx.enter_context(tc.tile_pool(name="norms", bufs=4))
        scratch = ctx.enter_context(tc.tile_pool(name="scratch", bufs=2))
        flipped = ctx.enter_context(tc.psum_pool(name="flipped", bufs=4))
        products = ctx.enter_context(tc.psum_pool(name="products", bufs=4))

        x_k_rows = keep.tile([P, P], BF16)
        nc.vector.memset(x_k_rows[:], 0.0)
        nc.sync.dma_start(out=x_k_rows[0:SLABS, :], in_=x_k.rearrange("(b p) -> b p", p=P))

        x_sb = keep.tile([P, B, TILES, C], BF16)
        w_sb = keep.tile([P, SLABS, C], BF16)
        k_k_bf = keep.tile([P, C], BF16)
        for g in range(PASSES):
            cols = slice(g * K_PASS, (g + 1) * K_PASS)
            nc.sync.dma_start(out=x_sb[:, 0, :, cols], in_=x_view[:, 0, :, cols])
            nc.sync.dma_start(out=w_sb[:, :, cols], in_=w_view[:, :, cols])
        nc.sync.dma_start(out=k_k_bf[:], in_=k_k.partition_broadcast(P))
        for s in range(1, B):
            for g in range(PASSES):
                cols = slice(g * K_PASS, (g + 1) * K_PASS)
                nc.sync.dma_start(out=x_sb[:, s, :, cols], in_=x_view[:, s, :, cols])

        ident = keep.tile([P, P], BF16)
        make_identity(nc, ident[:])

        one = keep.tile([P, 1], F32)
        nc.vector.memset(one[:], 1.0)
        nc.scalar.activation(out=one[:], in_=one[:], func=ACT.Abs_reciprocal_sqrt)

        x_k_flipped = flipped.tile([P, T], BF16, tag="bank")
        nc.tensor.transpose(x_k_flipped[:, 0:P], x_k_rows[:], ident[:])
        mix_prev = keep.tile([P, SLABS], F32)
        mix_here = keep.tile([P, SLABS], F32)
        nc.vector.tensor_copy(out=mix_prev[:], in_=x_k_flipped[:, 0:SLABS])
        nc.vector.tensor_scalar(
            out=mix_here[:], in0=mix_prev[:], scalar1=-1.0, scalar2=1.0, op0=ALU.mult, op1=ALU.add
        )

        prev_tiles = [keep.tile([P, T], F32, name="prev_%d" % n) for n in range(3)]
        for prev in prev_tiles:
            nc.vector.memset(prev[:, 0:8], 0.0)

        k_k_f32 = keep.tile([P, C], F32)
        w_codes = keep.tile([P, PASSES, C], U32, align_bytes=64)
        w_scales = keep.tile([P, PASSES, C], U8, align_bytes=64)

        w_banks, w_grouped = {}, {}
        x_banks, planes, grouped, xk_mx = {}, {}, {}, {}
        accs, scaled, stats, v_sums, s_sums, inverse = {}, {}, {}, {}, {}, {}

        def flip_weights(b):
            g, quarter = divmod(b, SLABS // PASSES)
            w_banks[b] = products.tile([P, T], BF16, tag="acc", name="w_bank")
            for r in range(2):
                for j in range(PACK):
                    slot = r * PACK + j
                    slab = g * PACK + j
                    nc.tensor.transpose(
                        w_banks[b][:, slot * P : (slot + 1) * P],
                        w_sb[:, quarter * 2 + r, slab * P : (slab + 1) * P],
                        ident[:],
                    )

        def group_weights(b):
            g, quarter = divmod(b, SLABS // PASSES)
            if quarter == 0:
                w_grouped[g] = w_stage.tile([P, C, PACK], BF16, align_bytes=64, name="w_grouped")
            nc.scalar.copy(
                out=w_grouped[g][:, quarter * 2 * P : (quarter + 1) * 2 * P, :].rearrange(
                    "p (r o) j -> p r o j", r=2
                ),
                in_=w_banks[b][:].rearrange("p (r j o) -> p r o j", r=2, j=PACK),
            )

        def quantise_weights(g):
            nc.vector.quantize_mx(
                out=w_codes[:, g, :].bitcast(FP8X4),
                scales=w_scales[:, g, :],
                in_=w_grouped[g][:].rearrange("p o j -> p (o j)"),
            )

        def flip(m):
            s, slab = divmod(m, SLABS)
            x_banks[m] = flipped.tile([P, T], BF16, tag="bank", name="x_bank")
            for i in range(TILES):
                nc.tensor.transpose(
                    x_banks[m][:, i * P : (i + 1) * P],
                    x_sb[:, s, i, slab * P : (slab + 1) * P],
                    ident[:],
                )

        def shift(m):
            slab = m % SLABS
            nc.scalar.activation(
                out=prev_tiles[m % len(prev_tiles)][:, 1:T],
                in_=x_banks[m][:, 0 : T - 1],
                func=ACT.Copy,
                scale=mix_prev[:, slab : slab + 1],
            )

        def blend(m):
            slab = m % SLABS
            q, j = divmod(m, PACK)
            if j == 0:
                planes[q] = mix_stage.tile([P, PACK, T], BF16, name="planes")
            nc.vector.scalar_tensor_tensor(
                out=planes[q][:, j, :],
                in0=x_banks[m][:],
                scalar=mix_here[:, slab : slab + 1],
                in1=prev_tiles[m % len(prev_tiles)][:],
                op0=ALU.mult,
                op1=ALU.add,
            )

        def regroup(q):
            grouped[q] = mix_stage.tile([P, T, PACK], BF16, align_bytes=64, name="grouped")
            nc.vector.tensor_copy(
                out=grouped[q][:].rearrange("p (c i) j -> p c j i", i=RUN),
                in_=planes[q][:].rearrange("p j (c i) -> p c j i", i=RUN),
            )

        def quantise(q):
            codes = quantised.tile([P, T], U32, align_bytes=64)
            scales = quantised.tile([P, T], U8, align_bytes=64)
            nc.vector.quantize_mx(
                out=codes[:].bitcast(FP8X4),
                scales=scales[:],
                in_=grouped[q][:].rearrange("p t j -> p (t j)"),
            )
            xk_mx[q] = (codes, scales)

        def multiply(n):
            s, i = divmod(n, TILES)
            tokens = slice(i * P, (i + 1) * P)
            accs[n] = []
            for half in range(N_TILES):
                cols = slice(half * N_TILE, (half + 1) * N_TILE)
                acc = products.tile([P, N_TILE], F32, tag="acc")
                for g in range(PASSES):
                    codes, scales = xk_mx[s * PASSES + g]
                    nc.tensor.matmul_mx(
                        out=acc[:],
                        lhsT=codes[:, tokens].bitcast(FP8X4),
                        lhsT_scale=scales[:, tokens],
                        rhs=w_codes[:, g, cols].bitcast(FP8X4),
                        rhs_scale=w_scales[:, g, cols],
                        start=(g == 0),
                        stop=(g == PASSES - 1),
                    )
                accs[n].append(acc)

        def times_k_k(n):
            pair, t = divmod(n, PAIR)
            if t == 0:
                scaled[pair] = results.tile([P, PAIR, C], F32, name="scaled")
            for half in range(N_TILES):
                cols = slice(half * N_TILE, (half + 1) * N_TILE)
                nc.vector.tensor_tensor(
                    out=scaled[pair][:, t, cols], in0=accs[n][half][:], in1=k_k_f32[:, cols], op=ALU.mult
                )

        def sum_squares_on_vector(n):
            pair, t = divmod(n, PAIR)
            if t == 0:
                stats[pair] = norms.tile([P, PAIR, V_HEADS, STATS], F32, name="stats")
            for h in range(0, V_HEADS, 2):
                nc.vector.bn_stats(
                    out=stats[pair][:, t, h : h + 2, :].rearrange("p h k -> p (h k)"),
                    in_=scaled[pair][:, t, h * HEAD : (h + 2) * HEAD].rearrange(
                        "p (h d) -> p d h", h=2
                    ),
                )

        def sum_squares_on_scalar(n):
            pair, t = divmod(n, PAIR)
            if t == 0:
                s_sums[pair] = norms.tile([P, PAIR, S_HEADS], F32, name="s_sums")
            squares = scratch.tile([P, S_HEADS * HEAD], BF16)
            for h in range(S_HEADS):
                nc.scalar.activation(
                    out=squares[:, h * HEAD : (h + 1) * HEAD],
                    in_=scaled[pair][:, t, (V_HEADS + h) * HEAD : (V_HEADS + h + 1) * HEAD],
                    func=ACT.Square,
                    accum_out=s_sums[pair][:, t, h : h + 1],
                )

        def finish_vector_sums(pair):
            mean = stats[pair][:, :, :, 1]
            mean_squared = norms.tile([P, PAIR, V_HEADS], F32)
            v_sums[pair] = norms.tile([P, PAIR, V_HEADS], F32, name="v_sums")
            nc.vector.tensor_tensor(out=mean_squared[:], in0=mean, in1=mean, op=ALU.mult)
            nc.vector.scalar_tensor_tensor(
                out=v_sums[pair][:],
                in0=mean_squared[:],
                scalar=float(HEAD),
                in1=stats[pair][:, :, :, 2],
                op0=ALU.mult,
                op1=ALU.add,
            )

        def invert_norms(pair):
            inverse[pair] = norms.tile([P, PAIR, HEADS], F32, name="inverse")
            for sums, heads in (
                (v_sums[pair], slice(0, V_HEADS)),
                (s_sums[pair], slice(V_HEADS, HEADS)),
            ):
                nc.scalar.activation(
                    out=inverse[pair][:, :, heads],
                    in_=sums[:],
                    func=ACT.Abs_reciprocal_sqrt,
                    bias=TINY,
                )

        def normalise_and_store(pair, engine):
            s, first = divmod(pair * PAIR, TILES)
            capped = inverse[pair][:].rearrange("p t h -> p (t h)")
            engine.tensor_scalar_min(out=capped, in0=capped, scalar1=1.0 / NORM_FLOOR)
            by_head = scaled[pair][:].rearrange("p t (h d) -> p (t h) d", d=HEAD)
            for t in range(PAIR):
                for piece in range(t * HEADS // PIECE_HEADS, (t + 1) * HEADS // PIECE_HEADS):
                    heads = slice(piece * PIECE_HEADS, (piece + 1) * PIECE_HEADS)
                    engine.tensor_tensor(
                        out=by_head[:, heads, :],
                        in0=by_head[:, heads, :],
                        in1=capped[:, heads].unsqueeze(2).to_broadcast([P, PIECE_HEADS, HEAD]),
                        op=ALU.mult,
                    )
                nc.sync.dma_start(out=out_view[:, s, first + t, :], in_=scaled[pair][:, t, :])

        def due(index, count):
            return 0 <= index < count

        for tick in range(TICKS):
            if due(tick, B * SLABS):
                flip(tick)
            if due(tick - W_LAG, SLABS):
                flip_weights(tick - W_LAG)
            if due(tick - MULTIPLY_LAG, B * TILES):
                multiply(tick - MULTIPLY_LAG)

            if due(tick - SHIFT_LAG, B * SLABS):
                shift(tick - SHIFT_LAG)
            if due(tick - W_LAG - SHIFT_LAG, SLABS):
                group_weights(tick - W_LAG - SHIFT_LAG)

            m = tick - BLEND_LAG
            b = tick - W_LAG - BLEND_LAG
            if due(m, B * SLABS):
                blend(m)
                if m % PACK == PACK - 1:
                    regroup(m // PACK)
            if tick == MULTIPLY_LAG:
                nc.vector.tensor_copy(out=k_k_f32[:], in_=k_k_bf[:])
            if due(tick - K_K_LAG, B * TILES):
                times_k_k(tick - K_K_LAG)
            if due(tick - V_SUMS_LAG, B * TILES):
                sum_squares_on_vector(tick - V_SUMS_LAG)
                if (tick - V_SUMS_LAG) % PAIR == PAIR - 1:
                    finish_vector_sums((tick - V_SUMS_LAG) // PAIR)
            if due(m, B * SLABS) and m % PACK == PACK - 1:
                quantise(m // PACK)
            if due(b, SLABS) and b % PACK == PACK - 1:
                quantise_weights(b // PACK)

            if due(tick - SUMS_LAG, B * TILES):
                sum_squares_on_scalar(tick - SUMS_LAG)
                if (tick - SUMS_LAG) % PAIR == PAIR - 1:
                    invert_norms((tick - SUMS_LAG) // PAIR)

            if due(tick - NORMALISE_LAG, B * TILES) and (tick - NORMALISE_LAG) % PAIR == PAIR - 1:
                last_sequence = tick - NORMALISE_LAG >= (B - 1) * TILES
                normalise_and_store(
                    (tick - NORMALISE_LAG) // PAIR, nc.vector if last_sequence else nc.gpsimd
                )
